import numpy as np
import ml_dtypes


def mxq(x, axis, fmt="e4m3"):
    dtype, down = {"e4m3": (ml_dtypes.float8_e4m3fn, 7), "e5m2": (ml_dtypes.float8_e5m2, 14)}[fmt]
    v = np.moveaxis(np.asarray(x, np.float32).astype(ml_dtypes.bfloat16).astype(np.float64), axis, -1)
    blocks = v.reshape(v.shape[:-1] + (-1, 32))
    amax = np.abs(blocks).max(-1, keepdims=True)
    byte = np.maximum(np.where(amax > 0, np.frexp(amax)[1] - 1 + 127, 0) - down, 1)
    scale = np.exp2(byte - 127.0)
    codes = (blocks / scale).astype(np.float32).astype(dtype).astype(np.float64)
    return np.moveaxis((codes * scale).reshape(v.shape), -1, axis)


WIDE = False


def mx_kscale(k):
    if not WIDE:
        return np.ones(k)
    levels = np.array([10, -10, 5, -5, 0])
    a = np.random.permutation(np.resize(levels, k // 512 * 4)).reshape(k // 512, 4)
    idx = np.arange(k)
    return np.exp2(a[idx // 512, idx % 128 // 32])


BF16 = ml_dtypes.bfloat16


def bf(x):
    return np.asarray(x, np.float32).astype(BF16)


def f64(x):
    return np.asarray(x).astype(np.float64)


B, CIN, P, COUT, W, H, HEADS = 16, 1024, 512, 256, 16, 32, 4
N = W * H
EPS = 1e-5


def bn(y, g, b, m, v):
    return (y - f64(m)[None, :, None]) * (f64(g) / np.sqrt(f64(v) + EPS))[None, :, None] + f64(b)[None, :, None]


def setup_inputs():
    s, t = mx_kscale(P), mx_kscale(CIN)
    return {
        "h_attn": bf(np.maximum(np.random.standard_normal((B, P, N)), 0.0) * s[None, :, None]),
        "x": bf(np.random.standard_normal((B, CIN, N)) * t[None, :, None]),
        "conv3_w": bf(np.random.standard_normal((COUT, P)) * 1.5 / np.sqrt(P) / s[None, :]),
        "bn3_g": bf(np.random.uniform(0.5, 1.5, COUT)),
        "bn3_b": bf(np.random.standard_normal(COUT) * 0.3),
        "bn3_m": bf(np.random.standard_normal(COUT) * 0.3),
        "bn3_v": bf(np.random.uniform(0.5, 1.5, COUT)),
        "sc_w": bf(np.random.standard_normal((COUT, CIN)) / np.sqrt(CIN) / t[None, :]),
        "sc_b": bf(np.random.standard_normal(COUT) * 0.3),
        "scbn_g": bf(np.random.uniform(0.5, 1.5, COUT)),
        "scbn_b": bf(np.random.standard_normal(COUT) * 0.3),
        "scbn_m": bf(np.random.standard_normal(COUT) * 0.3),
        "scbn_v": bf(np.random.uniform(0.5, 1.5, COUT)),
    }


def reference(h_attn, x, conv3_w, bn3_g, bn3_b, bn3_m, bn3_v, sc_w, sc_b, scbn_g, scbn_b, scbn_m, scbn_v):
    main = bn(mxq(f64(conv3_w), 1, "e4m3") @ mxq(f64(h_attn), 1, "e4m3"), bn3_g, bn3_b, bn3_m, bn3_v)
    short = (mxq(f64(sc_w), 1, "e4m3") @ mxq(f64(x), 1, "e4m3")) + f64(sc_b)[None, :, None]
    short = bn(short, scbn_g, scbn_b, scbn_m, scbn_v)
    return np.maximum(main + short, 0.0)

@@ -1,0 +1,280 @@
+from contextlib import ExitStack
+
+import concourse.mybir as mybir
+from concourse.masks import make_identity
+
+F32 = mybir.dt.float32
+BF16 = mybir.dt.bfloat16
+U32 = mybir.dt.uint32
+U8 = mybir.dt.uint8
+FP8X4 = mybir.dt.float8_e4m3fn_x4
+ALU = mybir.AluOpType
+ACT = mybir.ActivationFunctionType
+
+B, CIN, CMID, COUT, N = 16, 1024, 512, 256, 512
+P = 128
+EPS = 1e-5
+FLOPS = 2 * B * COUT * N * (CMID + CIN)
+
+MANUAL = True
+CV = 112
+NRAW = 6
+LOOKAHEAD = 4
+RELU_ON_GPSIMD = False
+STORE_ON_GPSIMD = False
+
+
+def tile_bottleneck_transformer_pb_t_kernel(
+    tc, h_attn, x, conv3_w, bn3_g, bn3_b, bn3_m, bn3_v, sc_w, sc_b, scbn_g, scbn_b, scbn_m, scbn_v, out
+):
+    nc = tc.nc
+    with ExitStack() as ctx:
+        const = ctx.enter_context(tc.tile_pool(name="const", bufs=1))
+        rawp = ctx.enter_context(tc.tile_pool(name="rawp", bufs=NRAW))
+        grpp = ctx.enter_context(tc.tile_pool(name="grpp", bufs=3))
+        codep = ctx.enter_context(tc.tile_pool(name="codep", bufs=3))
+        outp = ctx.enter_context(tc.tile_pool(name="outp", bufs=4))
+        psum = ctx.enter_context(tc.psum_pool(name="psum", bufs=2))
+        if MANUAL:
+            ctx.enter_context(tc.manual_schedule())
+
+        raws = {}
+        grps = {}
+        codes = {}
+        accs = {}
+        outs = {}
+
+        def load(b):
+            rawh = rawp.tile([P, 2048], BF16, name="rawh", tag="rawh")
+            rawx = rawp.tile([P, 4096], BF16, name="rawx", tag="rawx")
+            nc.sync.dma_start(out=rawh[:], in_=h_attn[b].rearrange("(p j) w -> p (j w)", j=4))
+            if b == 0:
+                for g in range(2):
+                    nc.sync.dma_start(
+                        out=rawx[:, 2048 * g : 2048 * g + 2048],
+                        in_=x[b, 512 * g : 512 * g + 512, :].rearrange("(p j) w -> p (j w)", j=4),
+                    )
+            else:
+                nc.sync.dma_start(
+                    out=rawx[:].rearrange("p (g e) -> p g e", g=2),
+                    in_=x[b].rearrange("(g p j) w -> p g (j w)", g=2, j=4),
+                )
+            raws[b] = (rawh, rawx)
+
+        def regroup(copy, dst, src, c0, c1):
+            copy(
+                out=dst.rearrange("p (c i t) -> p c t i", i=4, t=4)[:, c0 // 4 : c1 // 4],
+                in_=src.rearrange("p (t c i) -> p c t i", t=4, i=4)[:, c0 // 4 : c1 // 4],
+            )
+
+        def alloc_grp(b):
+            grph = grpp.tile([P, 2048], BF16, name="grph", tag="grph", align_bytes=64)
+            grpx = grpp.tile([P, 4096], BF16, name="grpx", tag="grpx", align_bytes=64)
+            grps[b] = (grph, grpx)
+
+        def regroup_s(b, cv):
+            rawh, rawx = raws[b]
+            grph, grpx = grps[b]
+            regroup(nc.scalar.copy, grpx[:, 0:2048], rawx[:, 0:2048], 0, N)
+            if cv < N:
+                regroup(nc.scalar.copy, grpx[:, 2048:4096], rawx[:, 2048:4096], cv, N)
+
+        def regroup_v(b, cv):
+            rawh, rawx = raws[b]
+            grph, grpx = grps[b]
+            regroup(nc.vector.tensor_copy, grph[:], rawh[:], 0, N)
+            regroup(nc.vector.tensor_copy, grpx[:, 2048:4096], rawx[:, 2048:4096], 0, cv)
+
+        def quant(b):
+            grph, grpx = grps[b]
+            ch = codep.tile([P, 512], U32, name="ch", tag="ch", align_bytes=64)
+            sh = codep.tile([P, 512], U8, name="sh", tag="sh", align_bytes=64)
+            cx = codep.tile([P, 1024], U32, name="cx", tag="cx", align_bytes=64)
+            sx = codep.tile([P, 1024], U8, name="sx", tag="sx", align_bytes=64)
+            nc.vector.quantize_mx(out=cx[:].bitcast(FP8X4), scales=sx[:], in_=grpx[:])
+            nc.vector.quantize_mx(out=ch[:].bitcast(FP8X4), scales=sh[:], in_=grph[:])
+            codes[b] = (ch, sh, cx, sx)
+
+        def mm(b):
+            ch, sh, cx, sx = codes[b]
+            shorts = []
+            mains = []
+            for m in range(2):
+                short = psum.tile([P, N], F32, name="short%d" % m, tag="short%d" % m)
+                for g in range(2):
+                    w0 = 256 * (g + 1) + 128 * m
+                    nc.tensor.matmul_mx(
+                        out=short[:],
+                        lhsT=wq[:, w0 : w0 + 128].bitcast(FP8X4),
+                        lhsT_scale=wsc[:, w0 : w0 + 128],
+                        rhs=cx[:, 512 * g : 512 * g + 512].bitcast(FP8X4),
+                        rhs_scale=sx[:, 512 * g : 512 * g + 512],
+                        start=(g == 0),
+                        stop=(g == 1),
+                    )
+                shorts.append(short)
+            for m in range(2):
+                main = psum.tile([P, N], F32, name="main%d" % m, tag="main%d" % m)
+                nc.tensor.matmul_mx(
+                    out=main[:],
+                    lhsT=wq[:, 128 * m : 128 * m + 128].bitcast(FP8X4),
+                    lhsT_scale=wsc[:, 128 * m : 128 * m + 128],
+                    rhs=ch[:].bitcast(FP8X4),
+                    rhs_scale=sh[:],
+                    start=True,
+                    stop=True,
+                )
+                mains.append(main)
+            accs[b] = mains + shorts
+
+        def e1(b):
+            ot = outp.tile([P, 2 * N], F32, name="ot", tag="ot")
+            outs[b] = ot
+            for m in range(2):
+                nc.scalar.activation(
+                    out=ot[:, N * m : N * m + N],
+                    in_=accs[b][2 + m][:],
+                    func=ACT.Identity,
+                    bias=cvec[:, m : m + 1],
+                    scale=avec[:, 2 + m : 3 + m],
+                )
+
+        def e2(b):
+            ot = outs[b]
+            for m in range(2):
+                nc.vector.scalar_tensor_tensor(
+                    out=ot[:, N * m : N * m + N],
+                    in0=accs[b][m][:],
+                    scalar=avec[:, m : m + 1],
+                    in1=ot[:, N * m : N * m + N],
+                    op0=ALU.mult,
+                    op1=ALU.add,
+                )
+
+        def e3(b):
+            ot = outs[b]
+            if RELU_ON_GPSIMD:
+                nc.gpsimd.tensor_scalar(out=ot[:], in0=ot[:], scalar1=0.0, scalar2=0.0, op0=ALU.max, op1=ALU.add)
+            else:
+                nc.vector.tensor_scalar_max(out=ot[:], in0=ot[:], scalar1=0.0)
+
+        def store(b):
+            eng = nc.gpsimd if STORE_ON_GPSIMD else nc.sync
+            eng.dma_start(out=out[b].rearrange("(p m) n -> p (m n)", m=2), in_=outs[b][:])
+
+        load(0)
+        warm = const.tile([P, 1], F32, name="warm")
+        nc.vector.memset(warm[:], 1.0)
+        vraw = const.tile([P, 256], BF16, name="vraw")
+        nc.vector.memset(vraw[:], 0.0)
+        ident = const.tile([P, P], F32, name="ident")
+        make_identity(nc, ident[:])
+        vecs = [bn3_g, scbn_g, bn3_v, scbn_v, bn3_m, scbn_m, bn3_b, scbn_b, sc_b]
+        for r in range(4):
+            nc.scalar.dma_start(out=vraw[r : r + 1, :], in_=vecs[r].rearrange("(o n) -> o n", o=1))
+        nc.scalar.sqrt(warm[:], warm[:])
+        w3raw = const.tile([P, 1024], BF16, name="w3raw")
+        wsraw = const.tile([P, 2048], BF16, name="wsraw")
+        nc.sync.dma_start(out=w3raw[:], in_=conv3_w.rearrange("(p m) k -> p (m k)", m=2))
+        nc.sync.dma_start(out=wsraw[:], in_=sc_w.rearrange("(p m) k -> p (m k)", m=2))
+        load(1)
+        for r in range(4, 9):
+            nc.sync.dma_start(out=vraw[r : r + 1, :], in_=vecs[r].rearrange("(o n) -> o n", o=1))
+        for b in range(2, LOOKAHEAD):
+            load(b)
+
+        wgrp = const.tile([P, 3072], BF16, name="wgrp", align_bytes=64)
+        wq = const.tile([P, 768], U32, name="wq", align_bytes=64)
+        wsc = const.tile([P, 768], U8, name="wsc", align_bytes=64)
+        vt = const.tile([P, 16], F32, name="vt")
+        vf = const.tile([P, 18], F32, name="vf")
+        sd = const.tile([P, 4], F32, name="sd")
+        avec = const.tile([P, 4], F32, name="avec")
+        prod = const.tile([P, 4], F32, name="prod")
+        bsum = const.tile([P, 2], F32, name="bsum")
+        cvec = const.tile([P, 2], F32, name="cvec")
+
+        wtags = ["main0", "main1", "short0"]
+        wps = []
+        vpss = []
+
+        def w_transposes():
+            w3f = w3raw[:].bitcast(F32)
+            wsf = wsraw[:].bitcast(F32)
+            for g in range(3):
+                ps = psum.tile([P, 512], F32, name="wps%d" % g, tag=wtags[g])
+                for m in range(2):
+                    for u in range(2):
+                        if g == 0:
+                            src = w3f[:, 256 * m + u : 256 * m + 256 : 2]
+                        else:
+                            base = 512 * m + 256 * (g - 1)
+                            src = wsf[:, base + u : base + 256 : 2]
+                        nc.tensor.transpose(ps[:, 128 * (2 * m + u) : 128 * (2 * m + u) + 128], src, ident[:])
+                wps.append(ps)
+            vps = psum.tile([P, P], F32, name="vps", tag="short1")
+            nc.tensor.transpose(vps[:], vraw[:].bitcast(F32), ident[:])
+            vpss.append(vps)
+
+        def w_evac(copy, g):
+            copy(
+                out=wgrp[:, 1024 * g : 1024 * g + 1024].bitcast(F32).rearrange("q (m c u) -> q m c u", m=2, u=2),
+                in_=wps[g][:].rearrange("q (m u c) -> q m c u", m=2, u=2),
+            )
+
+        def w_quant3():
+            nc.vector.quantize_mx(out=wq[:, 0:256].bitcast(FP8X4), scales=wsc[:, 0:256], in_=wgrp[:, 0:1024])
+
+        def w_quants():
+            nc.vector.quantize_mx(out=wq[:, 256:768].bitcast(FP8X4), scales=wsc[:, 256:768], in_=wgrp[:, 1024:3072])
+
+        def bn_a():
+            nc.vector.tensor_copy(out=vt[:, 0:9], in_=vpss[0][:, 0:9])
+            nc.vector.tensor_copy(out=vf[:], in_=vt[:, 0:9].bitcast(BF16))
+            nc.vector.tensor_scalar_add(out=sd[:], in0=vf[:, 4:8], scalar1=EPS)
+
+        def bn_s():
+            nc.scalar.sqrt(sd[:], sd[:])
+
+        def bn_b():
+            nc.vector.reciprocal(out=sd[:], in_=sd[:])
+            nc.vector.tensor_mul(out=avec[:], in0=vf[:, 0:4], in1=sd[:])
+            nc.vector.tensor_sub(out=vf[:, 10:12], in0=vf[:, 10:12], in1=vf[:, 16:18])
+            nc.vector.tensor_mul(out=prod[:], in0=vf[:, 8:12], in1=avec[:])
+            nc.vector.tensor_add(out=bsum[:], in0=vf[:, 12:14], in1=vf[:, 14:16])
+            nc.vector.tensor_sub(out=bsum[:], in0=bsum[:], in1=prod[:, 0:2])
+            nc.vector.tensor_sub(out=cvec[:], in0=bsum[:], in1=prod[:, 2:4])
+
+        w_transposes()
+        alloc_grp(0)
+        regroup_s(0, N)
+        regroup_v(0, N)
+        for g in range(3):
+            w_evac(nc.scalar.copy, g)
+        quant(0)
+        w_quant3()
+        alloc_grp(1)
+        regroup(nc.vector.tensor_copy, grps[1][0][:], raws[1][0][:], 0, N)
+        bn_a()
+        bn_s()
+        regroup_s(1, CV)
+        w_quants()
+        mm(0)
+        regroup(nc.vector.tensor_copy, grps[1][1][:, 2048:4096], raws[1][1][:, 2048:4096], 0, CV)
+        bn_b()
+
+        for i in range(1, B + 1):
+            j = i + LOOKAHEAD - 1
+            if j < B:
+                load(j)
+            e1(i - 1)
+            if i + 1 < B:
+                alloc_grp(i + 1)
+                regroup_s(i + 1, CV)
+                regroup_v(i + 1, CV)
+            if i < B:
+                quant(i)
+                mm(i)
+            e2(i - 1)
+            e3(i - 1)
+            store(i - 1)

@@ -14,13 +14,14 @@ ACT = mybir.ActivationFunctionType
 B, CIN, CMID, COUT, N = 16, 1024, 512, 256, 512
 P = 128
 EPS = 1e-5
+FLT_MAX = 3.4028234663852886e38
 FLOPS = 2 * B * COUT * N * (CMID + CIN)
 
 MANUAL = True
-CV = 112
-NRAW = 6
-LOOKAHEAD = 4
-RELU_ON_GPSIMD = False
+CV = 224
+NRAW = 7
+LOOKAHEAD = 5
+RELU_ON_GPSIMD = True
 STORE_ON_GPSIMD = False
 
 
@@ -154,7 +155,7 @@ def tile_bottleneck_transformer_pb_t_kernel(
         def e3(b):
             ot = outs[b]
             if RELU_ON_GPSIMD:
-                nc.gpsimd.tensor_scalar(out=ot[:], in0=ot[:], scalar1=0.0, scalar2=0.0, op0=ALU.max, op1=ALU.add)
+                nc.gpsimd.tensor_scalar(out=ot[:], in0=ot[:], scalar1=FLT_MAX, scalar2=0.0, op0=ALU.min, op1=ALU.max)
             else:
                 nc.vector.tensor_scalar_max(out=ot[:], in0=ot[:], scalar1=0.0)
 
@@ -245,6 +246,9 @@ def tile_bottleneck_transformer_pb_t_kernel(
             nc.vector.tensor_sub(out=bsum[:], in0=bsum[:], in1=prod[:, 0:2])
             nc.vector.tensor_sub(out=cvec[:], in0=bsum[:], in1=prod[:, 2:4])
 
+        def cv_of(b):
+            return N if (b <= 1 or b == B - 1) else CV
+
         w_transposes()
         alloc_grp(0)
         regroup_s(0, N)
@@ -257,10 +261,10 @@ def tile_bottleneck_transformer_pb_t_kernel(
         regroup(nc.vector.tensor_copy, grps[1][0][:], raws[1][0][:], 0, N)
         bn_a()
         bn_s()
-        regroup_s(1, CV)
+        regroup_s(1, N)
         w_quants()
         mm(0)
-        regroup(nc.vector.tensor_copy, grps[1][1][:, 2048:4096], raws[1][1][:, 2048:4096], 0, CV)
+        regroup(nc.vector.tensor_copy, grps[1][1][:, 2048:4096], raws[1][1][:, 2048:4096], 0, N)
         bn_b()
 
         for i in range(1, B + 1):
@@ -270,8 +274,8 @@ def tile_bottleneck_transformer_pb_t_kernel(
             e1(i - 1)
             if i + 1 < B:
                 alloc_grp(i + 1)
-                regroup_s(i + 1, CV)
-                regroup_v(i + 1, CV)
+                regroup_s(i + 1, cv_of(i + 1))
+                regroup_v(i + 1, cv_of(i + 1))
             if i < B:
                 quant(i)
                 mm(i)

@@ -18,7 +18,7 @@ FLT_MAX = 3.4028234663852886e38
 FLOPS = 2 * B * COUT * N * (CMID + CIN)
 
 MANUAL = True
-CV = 224
+CV = 176
 NRAW = 7
 LOOKAHEAD = 5
 RELU_ON_GPSIMD = True

@@ -18,9 +18,9 @@ FLT_MAX = 3.4028234663852886e38
 FLOPS = 2 * B * COUT * N * (CMID + CIN)
 
 MANUAL = True
-CV = 176
-NRAW = 7
-LOOKAHEAD = 5
+CV = 224
+NRAW = 8
+LOOKAHEAD = 6
 RELU_ON_GPSIMD = True
 STORE_ON_GPSIMD = False
 
@@ -73,12 +73,12 @@ def tile_bottleneck_transformer_pb_t_kernel(
             grpx = grpp.tile([P, 4096], BF16, name="grpx", tag="grpx", align_bytes=64)
             grps[b] = (grph, grpx)
 
-        def regroup_s(b, cv):
-            rawh, rawx = raws[b]
-            grph, grpx = grps[b]
-            regroup(nc.scalar.copy, grpx[:, 0:2048], rawx[:, 0:2048], 0, N)
+        def regroup_s0(b):
+            regroup(nc.scalar.copy, grps[b][1][:, 0:2048], raws[b][1][:, 0:2048], 0, N)
+
+        def regroup_s1(b, cv):
             if cv < N:
-                regroup(nc.scalar.copy, grpx[:, 2048:4096], rawx[:, 2048:4096], cv, N)
+                regroup(nc.scalar.copy, grps[b][1][:, 2048:4096], raws[b][1][:, 2048:4096], cv, N)
 
         def regroup_v(b, cv):
             rawh, rawx = raws[b]
@@ -140,17 +140,16 @@ def tile_bottleneck_transformer_pb_t_kernel(
                     scale=avec[:, 2 + m : 3 + m],
                 )
 
-        def e2(b):
+        def e2(b, m):
             ot = outs[b]
-            for m in range(2):
-                nc.vector.scalar_tensor_tensor(
-                    out=ot[:, N * m : N * m + N],
-                    in0=accs[b][m][:],
-                    scalar=avec[:, m : m + 1],
-                    in1=ot[:, N * m : N * m + N],
-                    op0=ALU.mult,
-                    op1=ALU.add,
-                )
+            nc.vector.scalar_tensor_tensor(
+                out=ot[:, N * m : N * m + N],
+                in0=accs[b][m][:],
+                scalar=avec[:, m : m + 1],
+                in1=ot[:, N * m : N * m + N],
+                op0=ALU.mult,
+                op1=ALU.add,
+            )
 
         def e3(b):
             ot = outs[b]
@@ -163,6 +162,10 @@ def tile_bottleneck_transformer_pb_t_kernel(
             eng = nc.gpsimd if STORE_ON_GPSIMD else nc.sync
             eng.dma_start(out=out[b].rearrange("(p m) n -> p (m n)", m=2), in_=outs[b][:])
 
+        w3raw = const.tile([P, 1024], BF16, name="w3raw")
+        wsraw = const.tile([P, 2048], BF16, name="wsraw")
+        nc.sync.dma_start(out=w3raw[:], in_=conv3_w.rearrange("(p m) k -> p (m k)", m=2))
+        nc.sync.dma_start(out=wsraw[:], in_=sc_w.rearrange("(p m) k -> p (m k)", m=2))
         load(0)
         warm = const.tile([P, 1], F32, name="warm")
         nc.vector.memset(warm[:], 1.0)
@@ -174,10 +177,6 @@ def tile_bottleneck_transformer_pb_t_kernel(
         for r in range(4):
             nc.scalar.dma_start(out=vraw[r : r + 1, :], in_=vecs[r].rearrange("(o n) -> o n", o=1))
         nc.scalar.sqrt(warm[:], warm[:])
-        w3raw = const.tile([P, 1024], BF16, name="w3raw")
-        wsraw = const.tile([P, 2048], BF16, name="wsraw")
-        nc.sync.dma_start(out=w3raw[:], in_=conv3_w.rearrange("(p m) k -> p (m k)", m=2))
-        nc.sync.dma_start(out=wsraw[:], in_=sc_w.rearrange("(p m) k -> p (m k)", m=2))
         load(1)
         for r in range(4, 9):
             nc.sync.dma_start(out=vraw[r : r + 1, :], in_=vecs[r].rearrange("(o n) -> o n", o=1))
@@ -247,38 +246,50 @@ def tile_bottleneck_transformer_pb_t_kernel(
             nc.vector.tensor_sub(out=cvec[:], in0=bsum[:], in1=prod[:, 2:4])
 
         def cv_of(b):
-            return N if (b <= 1 or b == B - 1) else CV
+            return N if (b == 0 or b == B - 1) else CV
 
         w_transposes()
-        alloc_grp(0)
-        regroup_s(0, N)
-        regroup_v(0, N)
         for g in range(3):
             w_evac(nc.scalar.copy, g)
-        quant(0)
         w_quant3()
-        alloc_grp(1)
-        regroup(nc.vector.tensor_copy, grps[1][0][:], raws[1][0][:], 0, N)
+        alloc_grp(0)
+        regroup_s0(0)
+        regroup(nc.vector.tensor_copy, grps[0][0][:], raws[0][0][:], 0, N)
+        w_quants()
+        regroup(nc.vector.tensor_copy, grps[0][1][:, 2048:4096], raws[0][1][:, 2048:4096], 0, N)
+        quant(0)
+        mm(0)
         bn_a()
         bn_s()
-        regroup_s(1, N)
-        w_quants()
-        mm(0)
-        regroup(nc.vector.tensor_copy, grps[1][1][:, 2048:4096], raws[1][1][:, 2048:4096], 0, N)
+        alloc_grp(1)
+        regroup_s0(1)
+        regroup_s1(1, CV)
+        regroup(nc.vector.tensor_copy, grps[1][0][:], raws[1][0][:], 0, N)
         bn_b()
+        regroup(nc.vector.tensor_copy, grps[1][1][:, 2048:4096], raws[1][1][:, 2048:4096], 0, CV)
 
         for i in range(1, B + 1):
             j = i + LOOKAHEAD - 1
             if j < B:
                 load(j)
-            e1(i - 1)
             if i + 1 < B:
                 alloc_grp(i + 1)
-                regroup_s(i + 1, cv_of(i + 1))
+                regroup_s1(i + 1, cv_of(i + 1))
+            e1(i - 1)
+            if i + 1 < B:
+                regroup_s0(i + 1)
                 regroup_v(i + 1, cv_of(i + 1))
             if i < B:
                 quant(i)
                 mm(i)
-            e2(i - 1)
-            e3(i - 1)
-            store(i - 1)
+            if i < B:
+                e2(i - 1, 0)
+                e2(i - 1, 1)
+                e3(i - 1)
+                store(i - 1)
+            else:
+                for m in range(2):
+                    e2(i - 1, m)
+                    half = outs[i - 1][:, N * m : N * m + N]
+                    nc.vector.tensor_scalar_max(out=half, in0=half, scalar1=0.0)
+                    nc.sync.dma_start(out=out[i - 1].rearrange("(p m) n -> p m n", m=2)[:, m, :], in_=half)

@@ -41,21 +41,34 @@ def tile_bottleneck_transformer_pb_t_kernel(
 
         raws = {}
         grps = {}
-        codes = {}
+        codesx = {}
+        codesh = {}
         accs = {}
         outs = {}
 
         def load(b):
             rawh = rawp.tile([P, 2048], BF16, name="rawh", tag="rawh")
             rawx = rawp.tile([P, 4096], BF16, name="rawx", tag="rawx")
-            nc.sync.dma_start(out=rawh[:], in_=h_attn[b].rearrange("(p j) w -> p (j w)", j=4))
-            if b == 0:
-                for g in range(2):
-                    nc.sync.dma_start(
-                        out=rawx[:, 2048 * g : 2048 * g + 2048],
-                        in_=x[b, 512 * g : 512 * g + 512, :].rearrange("(p j) w -> p (j w)", j=4),
-                    )
+
+            def load_h():
+                nc.sync.dma_start(out=rawh[:], in_=h_attn[b].rearrange("(p j) w -> p (j w)", j=4))
+
+            def load_x(g):
+                nc.sync.dma_start(
+                    out=rawx[:, 2048 * g : 2048 * g + 2048],
+                    in_=x[b, 512 * g : 512 * g + 512, :].rearrange("(p j) w -> p (j w)", j=4),
+                )
+
+            if b == 0 or b == 2:
+                load_h()
+                load_x(0)
+                load_x(1)
+            elif b == 1:
+                load_x(0)
+                load_h()
+                load_x(1)
             else:
+                load_h()
                 nc.sync.dma_start(
                     out=rawx[:].rearrange("p (g e) -> p g e", g=2),
                     in_=x[b].rearrange("(g p j) w -> p g (j w)", g=2, j=4),
@@ -86,18 +99,25 @@ def tile_bottleneck_transformer_pb_t_kernel(
             regroup(nc.vector.tensor_copy, grph[:], rawh[:], 0, N)
             regroup(nc.vector.tensor_copy, grpx[:, 2048:4096], rawx[:, 2048:4096], 0, cv)
 
-        def quant(b):
-            grph, grpx = grps[b]
-            ch = codep.tile([P, 512], U32, name="ch", tag="ch", align_bytes=64)
-            sh = codep.tile([P, 512], U8, name="sh", tag="sh", align_bytes=64)
+        def quant_x(b):
             cx = codep.tile([P, 1024], U32, name="cx", tag="cx", align_bytes=64)
             sx = codep.tile([P, 1024], U8, name="sx", tag="sx", align_bytes=64)
-            nc.vector.quantize_mx(out=cx[:].bitcast(FP8X4), scales=sx[:], in_=grpx[:])
-            nc.vector.quantize_mx(out=ch[:].bitcast(FP8X4), scales=sh[:], in_=grph[:])
-            codes[b] = (ch, sh, cx, sx)
+            nc.vector.quantize_mx(out=cx[:].bitcast(FP8X4), scales=sx[:], in_=grps[b][1][:])
+            codesx[b] = (cx, sx)
+
+        def quant_h(b):
+            ch = codep.tile([P, 512], U32, name="ch", tag="ch", align_bytes=64)
+            sh = codep.tile([P, 512], U8, name="sh", tag="sh", align_bytes=64)
+            nc.vector.quantize_mx(out=ch[:].bitcast(FP8X4), scales=sh[:], in_=grps[b][0][:])
+            codesh[b] = (ch, sh)
+
+        def quant(b):
+            quant_x(b)
+            quant_h(b)
 
         def mm(b):
-            ch, sh, cx, sx = codes[b]
+            ch, sh = codesh[b]
+            cx, sx = codesx[b]
             shorts = []
             mains = []
             for m in range(2):
@@ -212,6 +232,8 @@ def tile_bottleneck_transformer_pb_t_kernel(
                             src = wsf[:, base + u : base + 256 : 2]
                         nc.tensor.transpose(ps[:, 128 * (2 * m + u) : 128 * (2 * m + u) + 128], src, ident[:])
                 wps.append(ps)
+
+        def v_transpose():
             vps = psum.tile([P, P], F32, name="vps", tag="short1")
             nc.tensor.transpose(vps[:], vraw[:].bitcast(F32), ident[:])
             vpss.append(vps)
@@ -256,17 +278,18 @@ def tile_bottleneck_transformer_pb_t_kernel(
         regroup_s0(0)
         regroup(nc.vector.tensor_copy, grps[0][0][:], raws[0][0][:], 0, N)
         w_quants()
+        quant_h(0)
         regroup(nc.vector.tensor_copy, grps[0][1][:, 2048:4096], raws[0][1][:, 2048:4096], 0, N)
-        quant(0)
+        quant_x(0)
+        v_transpose()
         mm(0)
-        bn_a()
-        bn_s()
         alloc_grp(1)
         regroup_s0(1)
         regroup_s1(1, CV)
         regroup(nc.vector.tensor_copy, grps[1][0][:], raws[1][0][:], 0, N)
-        bn_b()
         regroup(nc.vector.tensor_copy, grps[1][1][:, 2048:4096], raws[1][1][:, 2048:4096], 0, CV)
+        bn_a()
+        bn_s()
 
         for i in range(1, B + 1):
             j = i + LOOKAHEAD - 1
@@ -274,11 +297,19 @@ def tile_bottleneck_transformer_pb_t_kernel(
                 load(j)
             if i + 1 < B:
                 alloc_grp(i + 1)
-                regroup_s1(i + 1, cv_of(i + 1))
-            e1(i - 1)
-            if i + 1 < B:
+            if i == 1:
                 regroup_s0(i + 1)
+                regroup_s1(i + 1, cv_of(i + 1))
                 regroup_v(i + 1, cv_of(i + 1))
+                bn_b()
+                e1(i - 1)
+            else:
+                if i + 1 < B:
+                    regroup_s1(i + 1, cv_of(i + 1))
+                e1(i - 1)
+                if i + 1 < B:
+                    regroup_s0(i + 1)
+                    regroup_v(i + 1, cv_of(i + 1))
             if i < B:
                 quant(i)
                 mm(i)
@@ -291,5 +322,10 @@ def tile_bottleneck_transformer_pb_t_kernel(
                 for m in range(2):
                     e2(i - 1, m)
                     half = outs[i - 1][:, N * m : N * m + N]
-                    nc.vector.tensor_scalar_max(out=half, in0=half, scalar1=0.0)
+                    if m == 0:
+                        nc.gpsimd.tensor_scalar(
+                            out=half, in0=half, scalar1=FLT_MAX, scalar2=0.0, op0=ALU.min, op1=ALU.max
+                        )
+                    else:
+                        nc.vector.tensor_scalar_max(out=half, in0=half, scalar1=0.0)
                     nc.sync.dma_start(out=out[i - 1].rearrange("(p m) n -> p m n", m=2)[:, m, :], in_=half)

@@ -18,7 +18,8 @@ FLT_MAX = 3.4028234663852886e38
 FLOPS = 2 * B * COUT * N * (CMID + CIN)
 
 MANUAL = True
-CV = 224
+CV = 184
+CP = 384
 NRAW = 8
 LOOKAHEAD = 6
 RELU_ON_GPSIMD = True
@@ -35,7 +36,8 @@ def tile_bottleneck_transformer_pb_t_kernel(
         grpp = ctx.enter_context(tc.tile_pool(name="grpp", bufs=3))
         codep = ctx.enter_context(tc.tile_pool(name="codep", bufs=3))
         outp = ctx.enter_context(tc.tile_pool(name="outp", bufs=4))
-        psum = ctx.enter_context(tc.psum_pool(name="psum", bufs=2))
+        psum = ctx.enter_context(tc.psum_pool(name="psum", bufs=3))
+        psip = ctx.enter_context(tc.psum_pool(name="psip", bufs=2))
         if MANUAL:
             ctx.enter_context(tc.manual_schedule())
 
@@ -45,6 +47,7 @@ def tile_bottleneck_transformer_pb_t_kernel(
         codesh = {}
         accs = {}
         outs = {}
+        ips = {}
 
         def load(b):
             rawh = rawp.tile([P, 2048], BF16, name="rawh", tag="rawh")
@@ -90,8 +93,24 @@ def tile_bottleneck_transformer_pb_t_kernel(
             regroup(nc.scalar.copy, grps[b][1][:, 0:2048], raws[b][1][:, 0:2048], 0, N)
 
         def regroup_s1(b, cv):
-            if cv < N:
-                regroup(nc.scalar.copy, grps[b][1][:, 2048:4096], raws[b][1][:, 2048:4096], cv, N)
+            if cv < CP:
+                regroup(nc.scalar.copy, grps[b][1][:, 2048:4096], raws[b][1][:, 2048:4096], cv, CP)
+
+        def regroup_pe(b):
+            ip = psip.tile([P, 4 * (N - CP)], BF16, name="ip", tag="ip")
+            rows = raws[b][1][:, 2048:4096].rearrange("p (t c) -> p c t", t=4)
+            for u in range((N - CP) // 128):
+                nc.tensor.matmul(
+                    out=ip[:, 512 * u : 512 * u + 512],
+                    lhsT=identb[:],
+                    rhs=rows[:, CP + 128 * u : CP + 128 * u + 128, :],
+                    start=True,
+                    stop=True,
+                )
+            ips[b] = ip
+
+        def regroup_sp(b):
+            nc.scalar.copy(out=grps[b][1][:, 2048 + 4 * CP : 4096].bitcast(F32), in_=ips[b][:].bitcast(F32))
 
         def regroup_v(b, cv):
             rawh, rawx = raws[b]
@@ -121,7 +140,7 @@ def tile_bottleneck_transformer_pb_t_kernel(
             shorts = []
             mains = []
             for m in range(2):
-                short = psum.tile([P, N], F32, name="short%d" % m, tag="short%d" % m)
+                short = psum.tile([P, N], F32, name="short%d" % m, tag="short")
                 for g in range(2):
                     w0 = 256 * (g + 1) + 128 * m
                     nc.tensor.matmul_mx(
@@ -135,7 +154,7 @@ def tile_bottleneck_transformer_pb_t_kernel(
                     )
                 shorts.append(short)
             for m in range(2):
-                main = psum.tile([P, N], F32, name="main%d" % m, tag="main%d" % m)
+                main = psum.tile([P, N], F32, name="main%d" % m, tag="main")
                 nc.tensor.matmul_mx(
                     out=main[:],
                     lhsT=wq[:, 128 * m : 128 * m + 128].bitcast(FP8X4),
@@ -193,6 +212,8 @@ def tile_bottleneck_transformer_pb_t_kernel(
         nc.vector.memset(vraw[:], 0.0)
         ident = const.tile([P, P], F32, name="ident")
         make_identity(nc, ident[:])
+        identb = const.tile([P, P], BF16, name="identb")
+        make_identity(nc, identb[:])
         vecs = [bn3_g, scbn_g, bn3_v, scbn_v, bn3_m, scbn_m, bn3_b, scbn_b, sc_b]
         for r in range(4):
             nc.scalar.dma_start(out=vraw[r : r + 1, :], in_=vecs[r].rearrange("(o n) -> o n", o=1))
@@ -214,7 +235,6 @@ def tile_bottleneck_transformer_pb_t_kernel(
         bsum = const.tile([P, 2], F32, name="bsum")
         cvec = const.tile([P, 2], F32, name="cvec")
 
-        wtags = ["main0", "main1", "short0"]
         wps = []
         vpss = []
 
@@ -222,7 +242,7 @@ def tile_bottleneck_transformer_pb_t_kernel(
             w3f = w3raw[:].bitcast(F32)
             wsf = wsraw[:].bitcast(F32)
             for g in range(3):
-                ps = psum.tile([P, 512], F32, name="wps%d" % g, tag=wtags[g])
+                ps = psum.tile([P, 512], F32, name="wps%d" % g, tag="main")
                 for m in range(2):
                     for u in range(2):
                         if g == 0:
@@ -234,7 +254,7 @@ def tile_bottleneck_transformer_pb_t_kernel(
                 wps.append(ps)
 
         def v_transpose():
-            vps = psum.tile([P, P], F32, name="vps", tag="short1")
+            vps = psum.tile([P, P], F32, name="vps", tag="short")
             nc.tensor.transpose(vps[:], vraw[:].bitcast(F32), ident[:])
             vpss.append(vps)
 
@@ -268,7 +288,7 @@ def tile_bottleneck_transformer_pb_t_kernel(
             nc.vector.tensor_sub(out=cvec[:], in0=bsum[:], in1=prod[:, 2:4])
 
         def cv_of(b):
-            return N if (b == 0 or b == B - 1) else CV
+            return CP if (b == 0 or b == B - 1) else CV
 
         w_transposes()
         for g in range(3):
@@ -279,13 +299,17 @@ def tile_bottleneck_transformer_pb_t_kernel(
         regroup(nc.vector.tensor_copy, grps[0][0][:], raws[0][0][:], 0, N)
         w_quants()
         quant_h(0)
-        regroup(nc.vector.tensor_copy, grps[0][1][:, 2048:4096], raws[0][1][:, 2048:4096], 0, N)
+        regroup(nc.vector.tensor_copy, grps[0][1][:, 2048:4096], raws[0][1][:, 2048:4096], 0, CP)
+        regroup_pe(0)
+        regroup_sp(0)
         quant_x(0)
         v_transpose()
+        regroup_pe(1)
         mm(0)
         alloc_grp(1)
         regroup_s0(1)
         regroup_s1(1, CV)
+        regroup_sp(1)
         regroup(nc.vector.tensor_copy, grps[1][0][:], raws[1][0][:], 0, N)
         regroup(nc.vector.tensor_copy, grps[1][1][:, 2048:4096], raws[1][1][:, 2048:4096], 0, CV)
         bn_a()
@@ -297,9 +321,11 @@ def tile_bottleneck_transformer_pb_t_kernel(
                 load(j)
             if i + 1 < B:
                 alloc_grp(i + 1)
+                regroup_pe(i + 1)
             if i == 1:
                 regroup_s0(i + 1)
                 regroup_s1(i + 1, cv_of(i + 1))
+                regroup_sp(i + 1)
                 regroup_v(i + 1, cv_of(i + 1))
                 bn_b()
                 e1(i - 1)
@@ -309,6 +335,7 @@ def tile_bottleneck_transformer_pb_t_kernel(
                 e1(i - 1)
                 if i + 1 < B:
                     regroup_s0(i + 1)
+                    regroup_sp(i + 1)
                     regroup_v(i + 1, cv_of(i + 1))
             if i < B:
                 quant(i)

from contextlib import ExitStack

import concourse.mybir as mybir
from concourse.masks import make_identity

F32 = mybir.dt.float32
BF16 = mybir.dt.bfloat16
U32 = mybir.dt.uint32
U8 = mybir.dt.uint8
FP8X4 = mybir.dt.float8_e4m3fn_x4
ALU = mybir.AluOpType
ACT = mybir.ActivationFunctionType

B, CIN, CMID, COUT, N = 16, 1024, 512, 256, 512
P = 128
EPS = 1e-5
FLT_MAX = 3.4028234663852886e38
FLOPS = 2 * B * COUT * N * (CMID + CIN)

MANUAL = True
CV = 184
CP = 384
NRAW = 8
LOOKAHEAD = 6
RELU_ON_GPSIMD = True
STORE_ON_GPSIMD = False


def tile_bottleneck_transformer_pb_t_kernel(
    tc, h_attn, x, conv3_w, bn3_g, bn3_b, bn3_m, bn3_v, sc_w, sc_b, scbn_g, scbn_b, scbn_m, scbn_v, out
):
    nc = tc.nc
    with ExitStack() as ctx:
        const = ctx.enter_context(tc.tile_pool(name="const", bufs=1))
        rawp = ctx.enter_context(tc.tile_pool(name="rawp", bufs=NRAW))
        grpp = ctx.enter_context(tc.tile_pool(name="grpp", bufs=3))
        codep = ctx.enter_context(tc.tile_pool(name="codep", bufs=3))
        outp = ctx.enter_context(tc.tile_pool(name="outp", bufs=4))
        psum = ctx.enter_context(tc.psum_pool(name="psum", bufs=3))
        psip = ctx.enter_context(tc.psum_pool(name="psip", bufs=2))
        if MANUAL:
            ctx.enter_context(tc.manual_schedule())

        raws = {}
        grps = {}
        codesx = {}
        codesh = {}
        accs = {}
        outs = {}
        ips = {}

        def load(b):
            rawh = rawp.tile([P, 2048], BF16, name="rawh", tag="rawh")
            rawx = rawp.tile([P, 4096], BF16, name="rawx", tag="rawx")

            def load_h():
                nc.sync.dma_start(out=rawh[:], in_=h_attn[b].rearrange("(p j) w -> p (j w)", j=4))

            def load_x(g):
                nc.sync.dma_start(
                    out=rawx[:, 2048 * g : 2048 * g + 2048],
                    in_=x[b, 512 * g : 512 * g + 512, :].rearrange("(p j) w -> p (j w)", j=4),
                )

            if b == 0 or b == 2:
                load_h()
                load_x(0)
                load_x(1)
            elif b == 1:
                load_x(0)
                load_h()
                load_x(1)
            else:
                load_h()
                nc.sync.dma_start(
                    out=rawx[:].rearrange("p (g e) -> p g e", g=2),
                    in_=x[b].rearrange("(g p j) w -> p g (j w)", g=2, j=4),
                )
            raws[b] = (rawh, rawx)

        def regroup(copy, dst, src, c0, c1):
            copy(
                out=dst.rearrange("p (c i t) -> p c t i", i=4, t=4)[:, c0 // 4 : c1 // 4],
                in_=src.rearrange("p (t c i) -> p c t i", t=4, i=4)[:, c0 // 4 : c1 // 4],
            )

        def alloc_grp(b):
            grph = grpp.tile([P, 2048], BF16, name="grph", tag="grph", align_bytes=64)
            grpx = grpp.tile([P, 4096], BF16, name="grpx", tag="grpx", align_bytes=64)
            grps[b] = (grph, grpx)

        def regroup_s0(b):
            regroup(nc.scalar.copy, grps[b][1][:, 0:2048], raws[b][1][:, 0:2048], 0, N)

        def regroup_s1(b, cv):
            if cv < CP:
                regroup(nc.scalar.copy, grps[b][1][:, 2048:4096], raws[b][1][:, 2048:4096], cv, CP)

        def regroup_pe(b):
            ip = psip.tile([P, 4 * (N - CP)], BF16, name="ip", tag="ip")
            rows = raws[b][1][:, 2048:4096].rearrange("p (t c) -> p c t", t=4)
            for u in range((N - CP) // 128):
                nc.tensor.matmul(
                    out=ip[:, 512 * u : 512 * u + 512],
                    lhsT=identb[:],
                    rhs=rows[:, CP + 128 * u : CP + 128 * u + 128, :],
                    start=True,
                    stop=True,
                )
            ips[b] = ip

        def regroup_sp(b):
            nc.scalar.copy(out=grps[b][1][:, 2048 + 4 * CP : 4096].bitcast(F32), in_=ips[b][:].bitcast(F32))

        def regroup_v(b, cv):
            rawh, rawx = raws[b]
            grph, grpx = grps[b]
            regroup(nc.vector.tensor_copy, grph[:], rawh[:], 0, N)
            regroup(nc.vector.tensor_copy, grpx[:, 2048:4096], rawx[:, 2048:4096], 0, cv)

        def quant_x(b):
            cx = codep.tile([P, 1024], U32, name="cx", tag="cx", align_bytes=64)
            sx = codep.tile([P, 1024], U8, name="sx", tag="sx", align_bytes=64)
            nc.vector.quantize_mx(out=cx[:].bitcast(FP8X4), scales=sx[:], in_=grps[b][1][:])
            codesx[b] = (cx, sx)

        def quant_h(b):
            ch = codep.tile([P, 512], U32, name="ch", tag="ch", align_bytes=64)
            sh = codep.tile([P, 512], U8, name="sh", tag="sh", align_bytes=64)
            nc.vector.quantize_mx(out=ch[:].bitcast(FP8X4), scales=sh[:], in_=grps[b][0][:])
            codesh[b] = (ch, sh)

        def quant(b):
            quant_x(b)
            quant_h(b)

        def mm(b):
            ch, sh = codesh[b]
            cx, sx = codesx[b]
            shorts = []
            mains = []
            for m in range(2):
                short = psum.tile([P, N], F32, name="short%d" % m, tag="short")
                for g in range(2):
                    w0 = 256 * (g + 1) + 128 * m
                    nc.tensor.matmul_mx(
                        out=short[:],
                        lhsT=wq[:, w0 : w0 + 128].bitcast(FP8X4),
                        lhsT_scale=wsc[:, w0 : w0 + 128],
                        rhs=cx[:, 512 * g : 512 * g + 512].bitcast(FP8X4),
                        rhs_scale=sx[:, 512 * g : 512 * g + 512],
                        start=(g == 0),
                        stop=(g == 1),
                    )
                shorts.append(short)
            for m in range(2):
                main = psum.tile([P, N], F32, name="main%d" % m, tag="main")
                nc.tensor.matmul_mx(
                    out=main[:],
                    lhsT=wq[:, 128 * m : 128 * m + 128].bitcast(FP8X4),
                    lhsT_scale=wsc[:, 128 * m : 128 * m + 128],
                    rhs=ch[:].bitcast(FP8X4),
                    rhs_scale=sh[:],
                    start=True,
                    stop=True,
                )
                mains.append(main)
            accs[b] = mains + shorts

        def e1(b):
            ot = outp.tile([P, 2 * N], F32, name="ot", tag="ot")
            outs[b] = ot
            for m in range(2):
                nc.scalar.activation(
                    out=ot[:, N * m : N * m + N],
                    in_=accs[b][2 + m][:],
                    func=ACT.Identity,
                    bias=cvec[:, m : m + 1],
                    scale=avec[:, 2 + m : 3 + m],
                )

        def e2(b, m):
            ot = outs[b]
            nc.vector.scalar_tensor_tensor(
                out=ot[:, N * m : N * m + N],
                in0=accs[b][m][:],
                scalar=avec[:, m : m + 1],
                in1=ot[:, N * m : N * m + N],
                op0=ALU.mult,
                op1=ALU.add,
            )

        def e3(b):
            ot = outs[b]
            if RELU_ON_GPSIMD:
                nc.gpsimd.tensor_scalar(out=ot[:], in0=ot[:], scalar1=FLT_MAX, scalar2=0.0, op0=ALU.min, op1=ALU.max)
            else:
                nc.vector.tensor_scalar_max(out=ot[:], in0=ot[:], scalar1=0.0)

        def store(b):
            eng = nc.gpsimd if STORE_ON_GPSIMD else nc.sync
            eng.dma_start(out=out[b].rearrange("(p m) n -> p (m n)", m=2), in_=outs[b][:])

        w3raw = const.tile([P, 1024], BF16, name="w3raw")
        wsraw = const.tile([P, 2048], BF16, name="wsraw")
        nc.sync.dma_start(out=w3raw[:], in_=conv3_w.rearrange("(p m) k -> p (m k)", m=2))
        nc.sync.dma_start(out=wsraw[:], in_=sc_w.rearrange("(p m) k -> p (m k)", m=2))
        load(0)
        warm = const.tile([P, 1], F32, name="warm")
        nc.vector.memset(warm[:], 1.0)
        vraw = const.tile([P, 256], BF16, name="vraw")
        nc.vector.memset(vraw[:], 0.0)
        ident = const.tile([P, P], F32, name="ident")
        make_identity(nc, ident[:])
        identb = const.tile([P, P], BF16, name="identb")
        make_identity(nc, identb[:])
        vecs = [bn3_g, scbn_g, bn3_v, scbn_v, bn3_m, scbn_m, bn3_b, scbn_b, sc_b]
        for r in range(4):
            nc.scalar.dma_start(out=vraw[r : r + 1, :], in_=vecs[r].rearrange("(o n) -> o n", o=1))
        nc.scalar.sqrt(warm[:], warm[:])
        load(1)
        for r in range(4, 9):
            nc.sync.dma_start(out=vraw[r : r + 1, :], in_=vecs[r].rearrange("(o n) -> o n", o=1))
        for b in range(2, LOOKAHEAD):
            load(b)

        wgrp = const.tile([P, 3072], BF16, name="wgrp", align_bytes=64)
        wq = const.tile([P, 768], U32, name="wq", align_bytes=64)
        wsc = const.tile([P, 768], U8, name="wsc", align_bytes=64)
        vt = const.tile([P, 16], F32, name="vt")
        vf = const.tile([P, 18], F32, name="vf")
        sd = const.tile([P, 4], F32, name="sd")
        avec = const.tile([P, 4], F32, name="avec")
        prod = const.tile([P, 4], F32, name="prod")
        bsum = const.tile([P, 2], F32, name="bsum")
        cvec = const.tile([P, 2], F32, name="cvec")

        wps = []
        vpss = []

        def w_transposes():
            w3f = w3raw[:].bitcast(F32)
            wsf = wsraw[:].bitcast(F32)
            for g in range(3):
                ps = psum.tile([P, 512], F32, name="wps%d" % g, tag="main")
                for m in range(2):
                    for u in range(2):
                        if g == 0:
                            src = w3f[:, 256 * m + u : 256 * m + 256 : 2]
                        else:
                            base = 512 * m + 256 * (g - 1)
                            src = wsf[:, base + u : base + 256 : 2]
                        nc.tensor.transpose(ps[:, 128 * (2 * m + u) : 128 * (2 * m + u) + 128], src, ident[:])
                wps.append(ps)

        def v_transpose():
            vps = psum.tile([P, P], F32, name="vps", tag="short")
            nc.tensor.transpose(vps[:], vraw[:].bitcast(F32), ident[:])
            vpss.append(vps)

        def w_evac(copy, g):
            copy(
                out=wgrp[:, 1024 * g : 1024 * g + 1024].bitcast(F32).rearrange("q (m c u) -> q m c u", m=2, u=2),
                in_=wps[g][:].rearrange("q (m u c) -> q m c u", m=2, u=2),
            )

        def w_quant3():
            nc.vector.quantize_mx(out=wq[:, 0:256].bitcast(FP8X4), scales=wsc[:, 0:256], in_=wgrp[:, 0:1024])

        def w_quants():
            nc.vector.quantize_mx(out=wq[:, 256:768].bitcast(FP8X4), scales=wsc[:, 256:768], in_=wgrp[:, 1024:3072])

        def bn_a():
            nc.vector.tensor_copy(out=vt[:, 0:9], in_=vpss[0][:, 0:9])
            nc.vector.tensor_copy(out=vf[:], in_=vt[:, 0:9].bitcast(BF16))
            nc.vector.tensor_scalar_add(out=sd[:], in0=vf[:, 4:8], scalar1=EPS)

        def bn_s():
            nc.scalar.sqrt(sd[:], sd[:])

        def bn_b():
            nc.vector.reciprocal(out=sd[:], in_=sd[:])
            nc.vector.tensor_mul(out=avec[:], in0=vf[:, 0:4], in1=sd[:])
            nc.vector.tensor_sub(out=vf[:, 10:12], in0=vf[:, 10:12], in1=vf[:, 16:18])
            nc.vector.tensor_mul(out=prod[:], in0=vf[:, 8:12], in1=avec[:])
            nc.vector.tensor_add(out=bsum[:], in0=vf[:, 12:14], in1=vf[:, 14:16])
            nc.vector.tensor_sub(out=bsum[:], in0=bsum[:], in1=prod[:, 0:2])
            nc.vector.tensor_sub(out=cvec[:], in0=bsum[:], in1=prod[:, 2:4])

        def cv_of(b):
            return CP if (b == 0 or b == B - 1) else CV

        w_transposes()
        for g in range(3):
            w_evac(nc.scalar.copy, g)
        w_quant3()
        alloc_grp(0)
        regroup_s0(0)
        regroup(nc.vector.tensor_copy, grps[0][0][:], raws[0][0][:], 0, N)
        w_quants()
        quant_h(0)
        regroup(nc.vector.tensor_copy, grps[0][1][:, 2048:4096], raws[0][1][:, 2048:4096], 0, CP)
        regroup_pe(0)
        regroup_sp(0)
        quant_x(0)
        v_transpose()
        regroup_pe(1)
        mm(0)
        alloc_grp(1)
        regroup_s0(1)
        regroup_s1(1, CV)
        regroup_sp(1)
        regroup(nc.vector.tensor_copy, grps[1][0][:], raws[1][0][:], 0, N)
        regroup(nc.vector.tensor_copy, grps[1][1][:, 2048:4096], raws[1][1][:, 2048:4096], 0, CV)
        bn_a()
        bn_s()

        for i in range(1, B + 1):
            j = i + LOOKAHEAD - 1
            if j < B:
                load(j)
            if i + 1 < B:
                alloc_grp(i + 1)
                regroup_pe(i + 1)
            if i == 1:
                regroup_s0(i + 1)
                regroup_s1(i + 1, cv_of(i + 1))
                regroup_sp(i + 1)
                regroup_v(i + 1, cv_of(i + 1))
                bn_b()
                e1(i - 1)
            else:
                if i + 1 < B:
                    regroup_s1(i + 1, cv_of(i + 1))
                e1(i - 1)
                if i + 1 < B:
                    regroup_s0(i + 1)
                    regroup_sp(i + 1)
                    regroup_v(i + 1, cv_of(i + 1))
            if i < B:
                quant(i)
                mm(i)
            if i < B:
                e2(i - 1, 0)
                e2(i - 1, 1)
                e3(i - 1)
                store(i - 1)
            else:
                for m in range(2):
                    e2(i - 1, m)
                    half = outs[i - 1][:, N * m : N * m + N]
                    if m == 0:
                        nc.gpsimd.tensor_scalar(
                            out=half, in0=half, scalar1=FLT_MAX, scalar2=0.0, op0=ALU.min, op1=ALU.max
                        )
                    else:
                        nc.vector.tensor_scalar_max(out=half, in0=half, scalar1=0.0)
                    nc.sync.dma_start(out=out[i - 1].rearrange("(p m) n -> p m n", m=2)[:, m, :], in_=half)
